import numpy as np
import ml_dtypes


def mxq(x, axis, fmt="e4m3"):
    dtype, down = {"e4m3": (ml_dtypes.float8_e4m3fn, 7), "e5m2": (ml_dtypes.float8_e5m2, 14)}[fmt]
    v = np.moveaxis(np.asarray(x, np.float32).astype(ml_dtypes.bfloat16).astype(np.float64), axis, -1)
    blocks = v.reshape(v.shape[:-1] + (-1, 32))
    amax = np.abs(blocks).max(-1, keepdims=True)
    byte = np.maximum(np.where(amax > 0, np.frexp(amax)[1] - 1 + 127, 0) - down, 1)
    scale = np.exp2(byte - 127.0)
    codes = (blocks / scale).astype(np.float32).astype(dtype).astype(np.float64)
    return np.moveaxis((codes * scale).reshape(v.shape), -1, axis)


WIDE = False


def mx_kscale(k):
    if not WIDE:
        return np.ones(k)
    levels = np.array([10, -10, 5, -5, 0])
    a = np.random.permutation(np.resize(levels, k // 512 * 4)).reshape(k // 512, 4)
    idx = np.arange(k)
    return np.exp2(a[idx // 512, idx % 128 // 32])


BF16 = ml_dtypes.bfloat16


def bf(x):
    return np.asarray(x, np.float32).astype(BF16)


def f64(x):
    return np.asarray(x).astype(np.float64)


B, N, E, L, A, H1, H2, G = 128, 8, 8, 128, 128, 1024, 8192, 8


def mish(v):
    return v * np.tanh(np.log(1.0 + np.exp(v)))


def simnorm(v):
    vg = v.reshape(v.shape[:-1] + (v.shape[-1] // G, G))
    ex = np.exp(vg - vg.max(-1, keepdims=True))
    return (ex / ex.sum(-1, keepdims=True)).reshape(v.shape)


def setup_inputs():
    s = mx_kscale(H2)
    r = np.random.standard_normal
    return {"h2": bf(mish(r((B, E, H2))) * s),
            "logits": bf(r((B, N, E))),
            "W3": bf(r((E, H2, L)) * 2.0 / np.sqrt(H2) / s[:, None]),
            "b3": bf(0.3 * r((E, L)))}


def reference(h2, logits, W3, b3):
    hq = mxq(f64(h2).transpose(1, 0, 2), 2, "e4m3")
    z = (hq @ mxq(f64(W3), 1, "e4m3")) + f64(b3)[:, None, :]
    y = simnorm(z)
    lg = f64(logits)
    ex = np.exp(lg - lg.max(-1, keepdims=True))
    comb = ex / ex.sum(-1, keepdims=True)
    return sum(comb[:, :, e, None] * y[e][:, None, :] for e in range(E))

@@ -1,0 +1,195 @@
+from contextlib import ExitStack
+
+import concourse.mybir as mybir
+from concourse.masks import make_identity
+
+F32 = mybir.dt.float32
+BF16 = mybir.dt.bfloat16
+U32 = mybir.dt.uint32
+U8 = mybir.dt.uint8
+FP8X4 = mybir.dt.float8_e4m3fn_x4
+ALU = mybir.AluOpType
+ACT = mybir.ActivationFunctionType
+AXIS_X = mybir.AxisListType.X
+
+P = 128
+PACK = 4
+K_PASS = P * PACK
+
+BATCH, AGENTS, EXPERTS, FEATURES, HIDDEN = 128, 8, 8, 128, 8192
+SIMNORM = 8
+GROUPS = FEATURES // SIMNORM
+
+CHUNK_PASSES = 8
+CHUNK_K = CHUNK_PASSES * K_PASS
+CHUNKS_PER_EXPERT = HIDDEN // CHUNK_K
+N_CHUNKS = EXPERTS * CHUNKS_PER_EXPERT
+BANK_PASSES = 2
+W_PASSES_ON_VECTOR = 4
+
+FLOPS = 2 * BATCH * EXPERTS * HIDDEN * FEATURES + 2 * BATCH * AGENTS * EXPERTS * FEATURES
+
+
+def tile_softmoedynamics_pb_k_kernel(tc, h2, logits, W3, b3, out):
+    nc = tc.nc
+    with ExitStack() as ctx:
+        consts = ctx.enter_context(tc.tile_pool(name="consts", bufs=1))
+        raw = ctx.enter_context(tc.tile_pool(name="raw", bufs=4))
+        grouped = ctx.enter_context(tc.tile_pool(name="grouped", bufs=3))
+        quantised = ctx.enter_context(tc.tile_pool(name="quantised", bufs=3))
+        small = ctx.enter_context(tc.tile_pool(name="small", bufs=2))
+        psum_t = ctx.enter_context(tc.psum_pool(name="psum_t", bufs=6))
+        psum_z = ctx.enter_context(tc.psum_pool(name="psum_z", bufs=2))
+
+        logits_sb = consts.tile([P, AGENTS, EXPERTS], BF16)
+        nc.scalar.dma_start(out=logits_sb[:], in_=logits)
+        bias_row = consts.tile([P, EXPERTS * FEATURES], BF16)
+        nc.vector.memset(bias_row[:], 0.0)
+        nc.scalar.dma_start(out=bias_row[0:1, :], in_=b3.rearrange("(o e) l -> o (e l)", o=1))
+        ones = consts.tile([P, P], BF16)
+        nc.vector.memset(ones[:], 1.0)
+        identity = consts.tile([P, P], F32)
+        make_identity(nc, identity[:])
+
+        def load_chunk(i):
+            e, half = divmod(i, CHUNKS_PER_EXPERT)
+            k0 = half * CHUNK_K
+            raw_h = raw.tile([P, CHUNK_K], BF16)
+            nc.sync.dma_start(out=raw_h[:], in_=h2[:, e, k0 : k0 + CHUNK_K])
+            raw_w = raw.tile([P, CHUNK_PASSES, PACK, FEATURES], BF16)
+            nc.sync.dma_start(
+                out=raw_w[:],
+                in_=W3[e, k0 : k0 + CHUNK_K, :].rearrange("(c p t) l -> p c t l", p=P, t=PACK),
+            )
+            return raw_h, raw_w
+
+        def transpose_h(raw_h):
+            words = raw_h[:].bitcast(F32).rearrange("p (c w u) -> p c u w", c=CHUNK_PASSES, u=2)
+            grouped_h = grouped.tile([P, CHUNK_PASSES * BATCH * PACK], BF16, align_bytes=64)
+            grouped_words = grouped_h[:].bitcast(F32).rearrange(
+                "p (c b u) -> p c b u", c=CHUNK_PASSES, u=2
+            )
+            for c0 in range(0, CHUNK_PASSES, BANK_PASSES):
+                bank = psum_t.tile([P, BANK_PASSES, 2, BATCH], F32, tag="bank")
+                for c in range(BANK_PASSES):
+                    for u in range(2):
+                        nc.tensor.transpose(bank[:, c, u, :], words[:, c0 + c, u, :], identity[:])
+                nc.scalar.copy(
+                    out=grouped_words[:, c0 : c0 + BANK_PASSES, :, :],
+                    in_=bank[:].rearrange("p c u b -> p c b u"),
+                )
+            return grouped_h
+
+        def regroup_w(raw_w):
+            grouped_w = grouped.tile([P, CHUNK_PASSES, FEATURES, PACK], BF16, align_bytes=64)
+            v = W_PASSES_ON_VECTOR
+            nc.vector.tensor_copy(
+                out=grouped_w[:, 0:v, :, :].rearrange("p c (q i) t -> p c q t i", i=4),
+                in_=raw_w[:, 0:v, :, :].rearrange("p c t (q i) -> p c q t i", i=4),
+            )
+            for c in range(v, CHUNK_PASSES):
+                nc.scalar.copy(
+                    out=grouped_w[:, c, :, :].rearrange("p (q i) t -> p q t i", i=4),
+                    in_=raw_w[:, c, :, :].rearrange("p t (q i) -> p q t i", i=4),
+                )
+            return grouped_w
+
+        def quantise(values, name):
+            codes = quantised.tile([P, CHUNK_PASSES * P], U32, align_bytes=64, name="codes_" + name)
+            scales = quantised.tile([P, CHUNK_PASSES * P], U8, align_bytes=64, name="scales_" + name)
+            nc.vector.quantize_mx(out=codes[:].bitcast(FP8X4), scales=scales[:], in_=values)
+            return codes, scales
+
+        def multiply(i, z, h_codes, h_scales, w_codes, w_scales):
+            half = i % CHUNKS_PER_EXPERT
+            for c in range(CHUNK_PASSES):
+                cols = slice(c * P, (c + 1) * P)
+                nc.tensor.matmul_mx(
+                    out=z[:],
+                    lhsT=h_codes[:, cols].bitcast(FP8X4),
+                    lhsT_scale=h_scales[:, cols],
+                    rhs=w_codes[:, cols].bitcast(FP8X4),
+                    rhs_scale=w_scales[:, cols],
+                    start=(half == 0 and c == 0),
+                    stop=(half == CHUNKS_PER_EXPERT - 1 and c == CHUNK_PASSES - 1),
+                )
+
+        bias_all = consts.tile([P, EXPERTS, FEATURES], F32)
+        bias_flat = bias_all[:].rearrange("p e l -> p (e l)")
+        for n0 in range(0, EXPERTS * FEATURES, 512):
+            bias_bank = psum_t.tile([P, 512], F32, tag="bank")
+            nc.tensor.matmul(
+                out=bias_bank[:], lhsT=ones[:], rhs=bias_row[:, n0 : n0 + 512], start=True, stop=True
+            )
+            nc.scalar.copy(out=bias_flat[:, n0 : n0 + 512], in_=bias_bank[:])
+
+        shape_ne = [P, AGENTS, EXPERTS]
+        logit_max = consts.tile([P, AGENTS], F32)
+        nc.vector.tensor_reduce(out=logit_max[:], in_=logits_sb[:], axis=AXIS_X, op=ALU.max)
+        comb = consts.tile(shape_ne, F32)
+        nc.vector.tensor_tensor(
+            out=comb[:], in0=logits_sb[:], in1=logit_max[:].unsqueeze(2).to_broadcast(shape_ne),
+            op=ALU.subtract,
+        )
+        nc.scalar.activation(out=comb[:], in_=comb[:], func=ACT.Exp)
+        logit_sum = consts.tile([P, AGENTS], F32)
+        nc.vector.tensor_reduce(out=logit_sum[:], in_=comb[:], axis=AXIS_X, op=ALU.add)
+        nc.vector.reciprocal(out=logit_sum[:], in_=logit_sum[:])
+        nc.vector.tensor_tensor(
+            out=comb[:], in0=comb[:], in1=logit_sum[:].unsqueeze(2).to_broadcast(shape_ne),
+            op=ALU.mult,
+        )
+
+        mixed = consts.tile([P, AGENTS, FEATURES], F32)
+
+        def epilogue(e, z):
+            shape_gi = [P, GROUPS, SIMNORM]
+            zb = small.tile(shape_gi, F32)
+            nc.vector.tensor_tensor(
+                out=zb[:].rearrange("p g i -> p (g i)"), in0=z[:], in1=bias_all[:, e, :], op=ALU.add
+            )
+            group_max = small.tile([P, GROUPS], F32)
+            nc.vector.tensor_reduce(out=group_max[:], in_=zb[:], axis=AXIS_X, op=ALU.max)
+            nc.vector.tensor_tensor(
+                out=zb[:], in0=zb[:], in1=group_max[:].unsqueeze(2).to_broadcast(shape_gi),
+                op=ALU.subtract,
+            )
+            y = small.tile(shape_gi, F32)
+            nc.scalar.activation(out=y[:], in_=zb[:], func=ACT.Exp)
+            group_sum = small.tile([P, GROUPS], F32)
+            nc.vector.tensor_reduce(out=group_sum[:], in_=y[:], axis=AXIS_X, op=ALU.add)
+            nc.vector.reciprocal(out=group_sum[:], in_=group_sum[:])
+            nc.vector.tensor_tensor(
+                out=y[:], in0=y[:], in1=group_sum[:].unsqueeze(2).to_broadcast(shape_gi), op=ALU.mult
+            )
+            y_flat = y[:].rearrange("p g i -> p (g i)")
+            for n in range(AGENTS):
+                weight = comb[:, n, e : e + 1]
+                if e == 0:
+                    nc.vector.tensor_scalar_mul(out=mixed[:, n, :], in0=y_flat, scalar1=weight)
+                else:
+                    nc.vector.scalar_tensor_tensor(
+                        out=mixed[:, n, :], in0=y_flat, scalar=weight, in1=mixed[:, n, :],
+                        op0=ALU.mult, op1=ALU.add,
+                    )
+
+        z = None
+        waiting = None
+        for i in range(N_CHUNKS + 1):
+            arrived = None
+            if i < N_CHUNKS:
+                raw_h, raw_w = load_chunk(i)
+                arrived = (transpose_h(raw_h), regroup_w(raw_w))
+            if waiting is not None:
+                grouped_h, grouped_w = waiting
+                h_codes, h_scales = quantise(grouped_h[:], "h")
+                w_codes, w_scales = quantise(grouped_w[:].rearrange("p c l t -> p (c l t)"), "w")
+                e, half = divmod(i - 1, CHUNKS_PER_EXPERT)
+                if half == 0:
+                    z = psum_z.tile([P, FEATURES], F32, name="z")
+                multiply(i - 1, z, h_codes, h_scales, w_codes, w_scales)
+                if half == CHUNKS_PER_EXPERT - 1:
+                    epilogue(e, z)
+            waiting = arrived
+
+        nc.sync.dma_start(out=out, in_=mixed[:])

@@ -33,8 +33,9 @@ FLOPS = 2 * BATCH * EXPERTS * HIDDEN * FEATURES + 2 * BATCH * AGENTS * EXPERTS *
 def tile_softmoedynamics_pb_k_kernel(tc, h2, logits, W3, b3, out):
     nc = tc.nc
     with ExitStack() as ctx:
+        ctx.enter_context(tc.manual_schedule())
         consts = ctx.enter_context(tc.tile_pool(name="consts", bufs=1))
-        raw = ctx.enter_context(tc.tile_pool(name="raw", bufs=4))
+        raw = ctx.enter_context(tc.tile_pool(name="raw", bufs=6))
         grouped = ctx.enter_context(tc.tile_pool(name="grouped", bufs=3))
         quantised = ctx.enter_context(tc.tile_pool(name="quantised", bufs=3))
         small = ctx.enter_context(tc.tile_pool(name="small", bufs=2))
@@ -42,10 +43,10 @@ def tile_softmoedynamics_pb_k_kernel(tc, h2, logits, W3, b3, out):
         psum_z = ctx.enter_context(tc.psum_pool(name="psum_z", bufs=2))
 
         logits_sb = consts.tile([P, AGENTS, EXPERTS], BF16)
-        nc.scalar.dma_start(out=logits_sb[:], in_=logits)
+        nc.sync.dma_start(out=logits_sb[:], in_=logits)
         bias_row = consts.tile([P, EXPERTS * FEATURES], BF16)
         nc.vector.memset(bias_row[:], 0.0)
-        nc.scalar.dma_start(out=bias_row[0:1, :], in_=b3.rearrange("(o e) l -> o (e l)", o=1))
+        nc.sync.dma_start(out=bias_row[0:1, :], in_=b3.rearrange("(o e) l -> o (e l)", o=1))
         ones = consts.tile([P, P], BF16)
         nc.vector.memset(ones[:], 1.0)
         identity = consts.tile([P, P], F32)
@@ -142,8 +143,9 @@ def tile_softmoedynamics_pb_k_kernel(tc, h2, logits, W3, b3, out):
 
         mixed = consts.tile([P, AGENTS, FEATURES], F32)
 
-        def epilogue(e, z):
-            shape_gi = [P, GROUPS, SIMNORM]
+        shape_gi = [P, GROUPS, SIMNORM]
+
+        def shift_by_group_max(e, z):
             zb = small.tile(shape_gi, F32)
             nc.vector.tensor_tensor(
                 out=zb[:].rearrange("p g i -> p (g i)"), in0=z[:], in1=bias_all[:, e, :], op=ALU.add
@@ -154,8 +156,14 @@ def tile_softmoedynamics_pb_k_kernel(tc, h2, logits, W3, b3, out):
                 out=zb[:], in0=zb[:], in1=group_max[:].unsqueeze(2).to_broadcast(shape_gi),
                 op=ALU.subtract,
             )
+            return zb
+
+        def exponential(zb):
             y = small.tile(shape_gi, F32)
             nc.scalar.activation(out=y[:], in_=zb[:], func=ACT.Exp)
+            return y
+
+        def normalise_and_mix(e, y):
             group_sum = small.tile([P, GROUPS], F32)
             nc.vector.tensor_reduce(out=group_sum[:], in_=y[:], axis=AXIS_X, op=ALU.add)
             nc.vector.reciprocal(out=group_sum[:], in_=group_sum[:])
@@ -173,23 +181,35 @@ def tile_softmoedynamics_pb_k_kernel(tc, h2, logits, W3, b3, out):
                         op0=ALU.mult, op1=ALU.add,
                     )
 
-        z = None
-        waiting = None
-        for i in range(N_CHUNKS + 1):
-            arrived = None
+        last_half = CHUNKS_PER_EXPERT - 1
+        regrouped = {}
+        operands = {}
+        sums = {}
+        exponentials = {}
+        for i in range(N_CHUNKS + 3):
+            e_mul, half_mul = divmod(i - 2, CHUNKS_PER_EXPERT)
+            e_mix, half_mix = divmod(i - 3, CHUNKS_PER_EXPERT)
+            if 0 <= i - 2 < N_CHUNKS:
+                if half_mul == 0:
+                    z = psum_z.tile([P, FEATURES], F32, name="z")
+                    sums[e_mul] = z
+                multiply(i - 2, sums[e_mul], *operands[i - 2])
             if i < N_CHUNKS:
                 raw_h, raw_w = load_chunk(i)
-                arrived = (transpose_h(raw_h), regroup_w(raw_w))
-            if waiting is not None:
-                grouped_h, grouped_w = waiting
-                h_codes, h_scales = quantise(grouped_h[:], "h")
-                w_codes, w_scales = quantise(grouped_w[:].rearrange("p c l t -> p (c l t)"), "w")
-                e, half = divmod(i - 1, CHUNKS_PER_EXPERT)
-                if half == 0:
-                    z = psum_z.tile([P, FEATURES], F32, name="z")
-                multiply(i - 1, z, h_codes, h_scales, w_codes, w_scales)
-                if half == CHUNKS_PER_EXPERT - 1:
-                    epilogue(e, z)
-            waiting = arrived
+                grouped_h = transpose_h(raw_h)
+            if 0 <= i - 1 < N_CHUNKS:
+                ready_h, ready_w = regrouped[i - 1]
+                operands[i - 1] = quantise(ready_h[:], "h") + quantise(
+                    ready_w[:].rearrange("p c l t -> p (c l t)"), "w"
+                )
+            starts_simnorm = 0 <= i - 2 < N_CHUNKS and half_mul == last_half
+            if starts_simnorm:
+                zb = shift_by_group_max(e_mul, sums[e_mul])
+            if 0 <= i - 3 < N_CHUNKS and half_mix == last_half:
+                normalise_and_mix(e_mix, exponentials[e_mix])
+            if i < N_CHUNKS:
+                regrouped[i] = (grouped_h, regroup_w(raw_w))
+            if starts_simnorm:
+                exponentials[e_mul] = exponential(zb)
 
         nc.sync.dma_start(out=out, in_=mixed[:])

@@ -20,196 +20,231 @@ BATCH, AGENTS, EXPERTS, FEATURES, HIDDEN = 128, 8, 8, 128, 8192
 SIMNORM = 8
 GROUPS = FEATURES // SIMNORM
 
-CHUNK_PASSES = 8
-CHUNK_K = CHUNK_PASSES * K_PASS
-CHUNKS_PER_EXPERT = HIDDEN // CHUNK_K
-N_CHUNKS = EXPERTS * CHUNKS_PER_EXPERT
+FIRST_EXPERT_UNITS = (2, 2, 4, 4, 4)
+EXPERT_UNITS = (4, 4, 4, 4)
+LAST_EXPERT_UNITS = (4, 4, 4, 2, 2)
 BANK_PASSES = 2
-W_PASSES_ON_VECTOR = 4
 
 FLOPS = 2 * BATCH * EXPERTS * HIDDEN * FEATURES + 2 * BATCH * AGENTS * EXPERTS * FEATURES
 
 
+def list_units():
+    units = []
+    for e in range(EXPERTS):
+        sizes = EXPERT_UNITS
+        if e == 0:
+            sizes = FIRST_EXPERT_UNITS
+        if e == EXPERTS - 1:
+            sizes = LAST_EXPERT_UNITS
+        c0 = 0
+        for n in sizes:
+            units.append((e, c0, n))
+            c0 += n
+    return units
+
+
 def tile_softmoedynamics_pb_k_kernel(tc, h2, logits, W3, b3, out):
     nc = tc.nc
+    units = list_units()
     with ExitStack() as ctx:
         ctx.enter_context(tc.manual_schedule())
         consts = ctx.enter_context(tc.tile_pool(name="consts", bufs=1))
-        raw = ctx.enter_context(tc.tile_pool(name="raw", bufs=6))
-        grouped = ctx.enter_context(tc.tile_pool(name="grouped", bufs=3))
-        quantised = ctx.enter_context(tc.tile_pool(name="quantised", bufs=3))
-        small = ctx.enter_context(tc.tile_pool(name="small", bufs=2))
+        raw = ctx.enter_context(tc.tile_pool(name="raw", bufs=12))
+        grouped = ctx.enter_context(tc.tile_pool(name="grouped", bufs=4))
+        quantised = ctx.enter_context(tc.tile_pool(name="quantised", bufs=4))
+        small = ctx.enter_context(tc.tile_pool(name="small", bufs=3))
         psum_t = ctx.enter_context(tc.psum_pool(name="psum_t", bufs=6))
         psum_z = ctx.enter_context(tc.psum_pool(name="psum_z", bufs=2))
 
-        logits_sb = consts.tile([P, AGENTS, EXPERTS], BF16)
-        nc.sync.dma_start(out=logits_sb[:], in_=logits)
-        bias_row = consts.tile([P, EXPERTS * FEATURES], BF16)
-        nc.vector.memset(bias_row[:], 0.0)
-        nc.sync.dma_start(out=bias_row[0:1, :], in_=b3.rearrange("(o e) l -> o (e l)", o=1))
-        ones = consts.tile([P, P], BF16)
-        nc.vector.memset(ones[:], 1.0)
-        identity = consts.tile([P, P], F32)
-        make_identity(nc, identity[:])
-
-        def load_chunk(i):
-            e, half = divmod(i, CHUNKS_PER_EXPERT)
-            k0 = half * CHUNK_K
-            raw_h = raw.tile([P, CHUNK_K], BF16)
-            nc.sync.dma_start(out=raw_h[:], in_=h2[:, e, k0 : k0 + CHUNK_K])
-            raw_w = raw.tile([P, CHUNK_PASSES, PACK, FEATURES], BF16)
+        def load(u):
+            e, c0, n = units[u]
+            k = slice(c0 * K_PASS, (c0 + n) * K_PASS)
+            raw_w = raw.tile([P, n, PACK, FEATURES], BF16)
             nc.sync.dma_start(
-                out=raw_w[:],
-                in_=W3[e, k0 : k0 + CHUNK_K, :].rearrange("(c p t) l -> p c t l", p=P, t=PACK),
+                out=raw_w[:], in_=W3[e, k, :].rearrange("(c p t) l -> p c t l", p=P, t=PACK)
             )
+            raw_h = raw.tile([P, n * K_PASS], BF16)
+            nc.sync.dma_start(out=raw_h[:], in_=h2[:, e, k])
             return raw_h, raw_w
 
-        def transpose_h(raw_h):
-            words = raw_h[:].bitcast(F32).rearrange("p (c w u) -> p c u w", c=CHUNK_PASSES, u=2)
-            grouped_h = grouped.tile([P, CHUNK_PASSES * BATCH * PACK], BF16, align_bytes=64)
-            grouped_words = grouped_h[:].bitcast(F32).rearrange(
-                "p (c b u) -> p c b u", c=CHUNK_PASSES, u=2
-            )
-            for c0 in range(0, CHUNK_PASSES, BANK_PASSES):
+        def transpose_h(u, raw_h):
+            n = units[u][2]
+            words = raw_h[:].bitcast(F32).rearrange("p (c w v) -> p c v w", c=n, v=2)
+            banks = []
+            for c0 in range(0, n, BANK_PASSES):
                 bank = psum_t.tile([P, BANK_PASSES, 2, BATCH], F32, tag="bank")
                 for c in range(BANK_PASSES):
-                    for u in range(2):
-                        nc.tensor.transpose(bank[:, c, u, :], words[:, c0 + c, u, :], identity[:])
+                    for v in range(2):
+                        nc.tensor.transpose(bank[:, c, v, :], words[:, c0 + c, v, :], identity[:])
+                banks.append(bank)
+            return banks
+
+        def group_h(u, banks, values):
+            n = units[u][2]
+            grouped_words = values[:, 0 : n * K_PASS].bitcast(F32).rearrange(
+                "p (c b v) -> p c b v", c=n, v=2
+            )
+            for j in range(len(banks)):
+                c0 = j * BANK_PASSES
                 nc.scalar.copy(
                     out=grouped_words[:, c0 : c0 + BANK_PASSES, :, :],
-                    in_=bank[:].rearrange("p c u b -> p c b u"),
+                    in_=banks[j][:].rearrange("p c v b -> p c b v"),
                 )
-            return grouped_h
 
-        def regroup_w(raw_w):
-            grouped_w = grouped.tile([P, CHUNK_PASSES, FEATURES, PACK], BF16, align_bytes=64)
-            v = W_PASSES_ON_VECTOR
-            nc.vector.tensor_copy(
-                out=grouped_w[:, 0:v, :, :].rearrange("p c (q i) t -> p c q t i", i=4),
-                in_=raw_w[:, 0:v, :, :].rearrange("p c t (q i) -> p c q t i", i=4),
+        def group_w(u, raw_w, values):
+            n = units[u][2]
+            on_vector = n // 2
+            grouped_w = values[:, n * K_PASS : 2 * n * K_PASS].rearrange(
+                "p (c l t) -> p c l t", c=n, t=PACK
             )
-            for c in range(v, CHUNK_PASSES):
+            nc.vector.tensor_copy(
+                out=grouped_w[:, 0:on_vector, :, :].rearrange("p c (q i) t -> p c q t i", i=4),
+                in_=raw_w[:, 0:on_vector, :, :].rearrange("p c t (q i) -> p c q t i", i=4),
+            )
+            for c in range(on_vector, n):
                 nc.scalar.copy(
                     out=grouped_w[:, c, :, :].rearrange("p (q i) t -> p q t i", i=4),
                     in_=raw_w[:, c, :, :].rearrange("p t (q i) -> p q t i", i=4),
                 )
-            return grouped_w
 
-        def quantise(values, name):
-            codes = quantised.tile([P, CHUNK_PASSES * P], U32, align_bytes=64, name="codes_" + name)
-            scales = quantised.tile([P, CHUNK_PASSES * P], U8, align_bytes=64, name="scales_" + name)
-            nc.vector.quantize_mx(out=codes[:].bitcast(FP8X4), scales=scales[:], in_=values)
+        def quantise(u, values):
+            n = units[u][2]
+            codes = quantised.tile([P, 2 * n * P], U32, align_bytes=64)
+            scales = quantised.tile([P, 2 * n * P], U8, align_bytes=64)
+            nc.vector.quantize_mx(out=codes[:].bitcast(FP8X4), scales=scales[:], in_=values[:])
             return codes, scales
 
-        def multiply(i, z, h_codes, h_scales, w_codes, w_scales):
-            half = i % CHUNKS_PER_EXPERT
-            for c in range(CHUNK_PASSES):
-                cols = slice(c * P, (c + 1) * P)
+        def multiply(u, z, codes, scales):
+            e, c0, n = units[u]
+            for c in range(n):
+                h_cols = slice(c * P, (c + 1) * P)
+                w_cols = slice((n + c) * P, (n + c + 1) * P)
                 nc.tensor.matmul_mx(
                     out=z[:],
-                    lhsT=h_codes[:, cols].bitcast(FP8X4),
-                    lhsT_scale=h_scales[:, cols],
-                    rhs=w_codes[:, cols].bitcast(FP8X4),
-                    rhs_scale=w_scales[:, cols],
-                    start=(half == 0 and c == 0),
-                    stop=(half == CHUNKS_PER_EXPERT - 1 and c == CHUNK_PASSES - 1),
+                    lhsT=codes[:, h_cols].bitcast(FP8X4),
+                    lhsT_scale=scales[:, h_cols],
+                    rhs=codes[:, w_cols].bitcast(FP8X4),
+                    rhs_scale=scales[:, w_cols],
+                    start=(c0 + c == 0),
+                    stop=(c0 + c == HIDDEN // K_PASS - 1),
                 )
 
+        loaded = {0: load(0), 1: load(1)}
+        logits_sb = consts.tile([P, AGENTS, EXPERTS], BF16)
+        nc.sync.dma_start(out=logits_sb[:], in_=logits)
+        identity = consts.tile([P, P], F32)
+        make_identity(nc, identity[:])
+        warm = consts.tile([P, 1], F32)
+        nc.gpsimd.memset(warm[:], 0.0)
+        nc.scalar.activation(out=warm[:], in_=warm[:], func=ACT.Exp)
+        bias_row = consts.tile([P, EXPERTS * FEATURES], BF16)
+        nc.gpsimd.memset(bias_row[:], 0.0)
+        nc.sync.dma_start(out=bias_row[0:1, :], in_=b3.rearrange("(o e) l -> o (e l)", o=1))
+        ones = consts.tile([P, P], BF16)
+        nc.gpsimd.memset(ones[:], 1.0)
+
         bias_all = consts.tile([P, EXPERTS, FEATURES], F32)
-        bias_flat = bias_all[:].rearrange("p e l -> p (e l)")
-        for n0 in range(0, EXPERTS * FEATURES, 512):
+        shape_ne = [P, AGENTS, EXPERTS]
+        logit_max = consts.tile([P, AGENTS], F32)
+        comb = consts.tile(shape_ne, F32)
+        logit_sum = consts.tile([P, AGENTS], F32)
+        mixed = consts.tile([P, AGENTS, FEATURES], F32)
+        shape_gi = [P, GROUPS, SIMNORM]
+
+        def spread_bias(n0):
             bias_bank = psum_t.tile([P, 512], F32, tag="bank")
             nc.tensor.matmul(
                 out=bias_bank[:], lhsT=ones[:], rhs=bias_row[:, n0 : n0 + 512], start=True, stop=True
             )
+            bias_flat = bias_all[:].rearrange("p e l -> p (e l)")
             nc.scalar.copy(out=bias_flat[:, n0 : n0 + 512], in_=bias_bank[:])
 
-        shape_ne = [P, AGENTS, EXPERTS]
-        logit_max = consts.tile([P, AGENTS], F32)
-        nc.vector.tensor_reduce(out=logit_max[:], in_=logits_sb[:], axis=AXIS_X, op=ALU.max)
-        comb = consts.tile(shape_ne, F32)
-        nc.vector.tensor_tensor(
-            out=comb[:], in0=logits_sb[:], in1=logit_max[:].unsqueeze(2).to_broadcast(shape_ne),
-            op=ALU.subtract,
-        )
-        nc.scalar.activation(out=comb[:], in_=comb[:], func=ACT.Exp)
-        logit_sum = consts.tile([P, AGENTS], F32)
-        nc.vector.tensor_reduce(out=logit_sum[:], in_=comb[:], axis=AXIS_X, op=ALU.add)
-        nc.vector.reciprocal(out=logit_sum[:], in_=logit_sum[:])
-        nc.vector.tensor_tensor(
-            out=comb[:], in0=comb[:], in1=logit_sum[:].unsqueeze(2).to_broadcast(shape_ne),
-            op=ALU.mult,
-        )
+        later = {}
 
-        mixed = consts.tile([P, AGENTS, FEATURES], F32)
+        def at(step, function):
+            later.setdefault(step, []).append(function)
 
-        shape_gi = [P, GROUPS, SIMNORM]
+        def run(step):
+            for function in later.get(step, []):
+                function()
 
-        def shift_by_group_max(e, z):
-            zb = small.tile(shape_gi, F32)
-            nc.vector.tensor_tensor(
-                out=zb[:].rearrange("p g i -> p (g i)"), in0=z[:], in1=bias_all[:, e, :], op=ALU.add
-            )
-            group_max = small.tile([P, GROUPS], F32)
-            nc.vector.tensor_reduce(out=group_max[:], in_=zb[:], axis=AXIS_X, op=ALU.max)
-            nc.vector.tensor_tensor(
-                out=zb[:], in0=zb[:], in1=group_max[:].unsqueeze(2).to_broadcast(shape_gi),
-                op=ALU.subtract,
-            )
-            return zb
+        def schedule_comb(step):
+            at(step, lambda: nc.vector.tensor_reduce(
+                out=logit_max[:], in_=logits_sb[:], axis=AXIS_X, op=ALU.max))
+            at(step + 1, lambda: nc.vector.tensor_tensor(
+                out=comb[:], in0=logits_sb[:], in1=logit_max[:].unsqueeze(2).to_broadcast(shape_ne),
+                op=ALU.subtract))
+            at(step + 3, lambda: nc.scalar.activation(out=comb[:], in_=comb[:], func=ACT.Exp))
+            at(step + 5, lambda: nc.vector.tensor_reduce(
+                out=logit_sum[:], in_=comb[:], axis=AXIS_X, op=ALU.add))
+            at(step + 6, lambda: nc.vector.reciprocal(out=logit_sum[:], in_=logit_sum[:]))
+            at(step + 7, lambda: nc.vector.tensor_tensor(
+                out=comb[:], in0=comb[:], in1=logit_sum[:].unsqueeze(2).to_broadcast(shape_ne),
+                op=ALU.mult))
 
-        def exponential(zb):
-            y = small.tile(shape_gi, F32)
-            nc.scalar.activation(out=y[:], in_=zb[:], func=ACT.Exp)
-            return y
-
-        def normalise_and_mix(e, y):
-            group_sum = small.tile([P, GROUPS], F32)
-            nc.vector.tensor_reduce(out=group_sum[:], in_=y[:], axis=AXIS_X, op=ALU.add)
-            nc.vector.reciprocal(out=group_sum[:], in_=group_sum[:])
-            nc.vector.tensor_tensor(
-                out=y[:], in0=y[:], in1=group_sum[:].unsqueeze(2).to_broadcast(shape_gi), op=ALU.mult
-            )
+        def mix(e, n, y):
             y_flat = y[:].rearrange("p g i -> p (g i)")
-            for n in range(AGENTS):
-                weight = comb[:, n, e : e + 1]
-                if e == 0:
-                    nc.vector.tensor_scalar_mul(out=mixed[:, n, :], in0=y_flat, scalar1=weight)
-                else:
-                    nc.vector.scalar_tensor_tensor(
-                        out=mixed[:, n, :], in0=y_flat, scalar=weight, in1=mixed[:, n, :],
-                        op0=ALU.mult, op1=ALU.add,
-                    )
+            weight = comb[:, n, e : e + 1]
+            if e == 0:
+                nc.vector.tensor_scalar_mul(out=mixed[:, n, :], in0=y_flat, scalar1=weight)
+            else:
+                nc.vector.scalar_tensor_tensor(
+                    out=mixed[:, n, :], in0=y_flat, scalar=weight, in1=mixed[:, n, :],
+                    op0=ALU.mult, op1=ALU.add,
+                )
+            if e == EXPERTS - 1 and n % 4 == 3:
+                nc.sync.dma_start(out=out[:, n - 3 : n + 1, :], in_=mixed[:, n - 3 : n + 1, :])
 
-        last_half = CHUNKS_PER_EXPERT - 1
-        regrouped = {}
+        def schedule_expert(step, e, z):
+            y = small.tile(shape_gi, F32)
+            group_max = small.tile([P, GROUPS], F32)
+            group_sum = small.tile([P, GROUPS], F32)
+            at(step, lambda: nc.vector.tensor_tensor(
+                out=y[:].rearrange("p g i -> p (g i)"), in0=z[:], in1=bias_all[:, e, :], op=ALU.add))
+            at(step + 1, lambda: nc.vector.tensor_reduce(
+                out=group_max[:], in_=y[:], axis=AXIS_X, op=ALU.max))
+            at(step + 2, lambda: nc.vector.tensor_tensor(
+                out=y[:], in0=y[:], in1=group_max[:].unsqueeze(2).to_broadcast(shape_gi),
+                op=ALU.subtract))
+            at(step + 4, lambda: nc.scalar.activation(out=y[:], in_=y[:], func=ACT.Exp))
+            at(step + 6, lambda: nc.vector.tensor_reduce(
+                out=group_sum[:], in_=y[:], axis=AXIS_X, op=ALU.add))
+            at(step + 7, lambda: nc.vector.reciprocal(out=group_sum[:], in_=group_sum[:]))
+            at(step + 8, lambda: nc.vector.tensor_tensor(
+                out=y[:], in0=y[:], in1=group_sum[:].unsqueeze(2).to_broadcast(shape_gi),
+                op=ALU.mult))
+            for n in range(AGENTS):
+                at(step + 9 + n, lambda n=n: mix(e, n, y))
+
+        schedule_comb(2)
+        at(4, lambda: spread_bias(0))
+        at(6, lambda: spread_bias(512))
+        banks = {0: transpose_h(0, loaded[0][0])}
+        ready = {}
         operands = {}
         sums = {}
-        exponentials = {}
-        for i in range(N_CHUNKS + 3):
-            e_mul, half_mul = divmod(i - 2, CHUNKS_PER_EXPERT)
-            e_mix, half_mix = divmod(i - 3, CHUNKS_PER_EXPERT)
-            if 0 <= i - 2 < N_CHUNKS:
-                if half_mul == 0:
+        for i in range(len(units) + 2):
+            if i >= 2:
+                e, c0, n = units[i - 2]
+                if c0 == 0:
                     z = psum_z.tile([P, FEATURES], F32, name="z")
-                    sums[e_mul] = z
-                multiply(i - 2, sums[e_mul], *operands[i - 2])
-            if i < N_CHUNKS:
-                raw_h, raw_w = load_chunk(i)
-                grouped_h = transpose_h(raw_h)
-            if 0 <= i - 1 < N_CHUNKS:
-                ready_h, ready_w = regrouped[i - 1]
-                operands[i - 1] = quantise(ready_h[:], "h") + quantise(
-                    ready_w[:].rearrange("p c l t -> p (c l t)"), "w"
-                )
-            starts_simnorm = 0 <= i - 2 < N_CHUNKS and half_mul == last_half
-            if starts_simnorm:
-                zb = shift_by_group_max(e_mul, sums[e_mul])
-            if 0 <= i - 3 < N_CHUNKS and half_mix == last_half:
-                normalise_and_mix(e_mix, exponentials[e_mix])
-            if i < N_CHUNKS:
-                regrouped[i] = (grouped_h, regroup_w(raw_w))
-            if starts_simnorm:
-                exponentials[e_mul] = exponential(zb)
-
-        nc.sync.dma_start(out=out, in_=mixed[:])
+                    sums[e] = z
+                multiply(i - 2, sums[e], *operands[i - 2])
+                if c0 + n == HIDDEN // K_PASS:
+                    schedule_expert(2 * i + 1, e, sums[e])
+            if i + 1 < len(units):
+                if i + 1 not in loaded:
+                    loaded[i + 1] = load(i + 1)
+                banks[i + 1] = transpose_h(i + 1, loaded[i + 1][0])
+            if i < len(units):
+                values = grouped.tile([P, 2 * units[i][2] * K_PASS], BF16, align_bytes=64)
+                ready[i] = values
+                group_w(i, loaded[i][1], values)
+            run(2 * i)
+            if i < len(units):
+                group_h(i, banks[i], ready[i])
+            if 1 <= i <= len(units):
+                operands[i - 1] = quantise(i - 1, ready[i - 1])
+            run(2 * i + 1)
+        for step in range(2 * (len(units) + 2), max(later) + 1):
+            run(step)

@@ -23,6 +23,7 @@ GROUPS = FEATURES // SIMNORM
 FIRST_EXPERT_UNITS = (2, 2, 4, 4, 4)
 EXPERT_UNITS = (4, 4, 4, 4)
 LAST_EXPERT_UNITS = (4, 4, 4, 2, 2)
+VECTOR_COLUMNS = 72
 BANK_PASSES = 2
 
 FLOPS = 2 * BATCH * EXPERTS * HIDDEN * FEATURES + 2 * BATCH * AGENTS * EXPERTS * FEATURES
@@ -93,19 +94,18 @@ def tile_softmoedynamics_pb_k_kernel(tc, h2, logits, W3, b3, out):
 
         def group_w(u, raw_w, values):
             n = units[u][2]
-            on_vector = n // 2
+            v = VECTOR_COLUMNS
             grouped_w = values[:, n * K_PASS : 2 * n * K_PASS].rearrange(
                 "p (c l t) -> p c l t", c=n, t=PACK
             )
             nc.vector.tensor_copy(
-                out=grouped_w[:, 0:on_vector, :, :].rearrange("p c (q i) t -> p c q t i", i=4),
-                in_=raw_w[:, 0:on_vector, :, :].rearrange("p c t (q i) -> p c q t i", i=4),
+                out=grouped_w[:, :, 0:v, :].rearrange("p c (q i) t -> p c q t i", i=4),
+                in_=raw_w[:, :, :, 0:v].rearrange("p c t (q i) -> p c q t i", i=4),
             )
-            for c in range(on_vector, n):
-                nc.scalar.copy(
-                    out=grouped_w[:, c, :, :].rearrange("p (q i) t -> p q t i", i=4),
-                    in_=raw_w[:, c, :, :].rearrange("p t (q i) -> p q t i", i=4),
-                )
+            nc.scalar.copy(
+                out=grouped_w[:, :, v:FEATURES, :].rearrange("p c (q i) t -> p c q t i", i=4),
+                in_=raw_w[:, :, :, v:FEATURES].rearrange("p c t (q i) -> p c q t i", i=4),
+            )
 
         def quantise(u, values):
             n = units[u][2]

@@ -20,10 +20,14 @@ BATCH, AGENTS, EXPERTS, FEATURES, HIDDEN = 128, 8, 8, 128, 8192
 SIMNORM = 8
 GROUPS = FEATURES // SIMNORM
 
+EXPERT_SETS = ((0, 1), (2, 3), (4, 5), (6,), (7,))
+PSUM_AGENTS = 4
+MIXES_PER_STEP = 2
+
 FIRST_EXPERT_UNITS = (2, 2, 4, 4, 4)
 EXPERT_UNITS = (4, 4, 4, 4)
 LAST_EXPERT_UNITS = (4, 4, 4, 2, 2)
-VECTOR_COLUMNS = 72
+VECTOR_COLUMNS = 76
 BANK_PASSES = 2
 
 FLOPS = 2 * BATCH * EXPERTS * HIDDEN * FEATURES + 2 * BATCH * AGENTS * EXPERTS * FEATURES
@@ -54,7 +58,8 @@ def tile_softmoedynamics_pb_k_kernel(tc, h2, logits, W3, b3, out):
         grouped = ctx.enter_context(tc.tile_pool(name="grouped", bufs=4))
         quantised = ctx.enter_context(tc.tile_pool(name="quantised", bufs=4))
         small = ctx.enter_context(tc.tile_pool(name="small", bufs=3))
-        psum_t = ctx.enter_context(tc.psum_pool(name="psum_t", bufs=6))
+        psum_t = ctx.enter_context(tc.psum_pool(name="psum_t", bufs=5))
+        psum_mix = ctx.enter_context(tc.psum_pool(name="psum_mix", bufs=1))
         psum_z = ctx.enter_context(tc.psum_pool(name="psum_z", bufs=2))
 
         def load(u):
@@ -120,7 +125,7 @@ def tile_softmoedynamics_pb_k_kernel(tc, h2, logits, W3, b3, out):
                 h_cols = slice(c * P, (c + 1) * P)
                 w_cols = slice((n + c) * P, (n + c + 1) * P)
                 nc.tensor.matmul_mx(
-                    out=z[:],
+                    out=z,
                     lhsT=codes[:, h_cols].bitcast(FP8X4),
                     lhsT_scale=scales[:, h_cols],
                     rhs=codes[:, w_cols].bitcast(FP8X4),
@@ -149,7 +154,7 @@ def tile_softmoedynamics_pb_k_kernel(tc, h2, logits, W3, b3, out):
         comb = consts.tile(shape_ne, F32)
         logit_sum = consts.tile([P, AGENTS], F32)
         mixed = consts.tile([P, AGENTS, FEATURES], F32)
-        shape_gi = [P, GROUPS, SIMNORM]
+        psum_mixed = psum_mix.tile([P, PSUM_AGENTS, FEATURES], F32)
 
         def spread_bias(n0):
             bias_bank = psum_t.tile([P, 512], F32, tag="bank")
@@ -183,38 +188,82 @@ def tile_softmoedynamics_pb_k_kernel(tc, h2, logits, W3, b3, out):
                 op=ALU.mult))
 
         def mix(e, n, y):
-            y_flat = y[:].rearrange("p g i -> p (g i)")
             weight = comb[:, n, e : e + 1]
             if e == 0:
-                nc.vector.tensor_scalar_mul(out=mixed[:, n, :], in0=y_flat, scalar1=weight)
+                nc.vector.tensor_scalar_mul(out=mixed[:, n, :], in0=y, scalar1=weight)
             else:
+                before = psum_mixed[:, n, :] if n < PSUM_AGENTS else mixed[:, n, :]
                 nc.vector.scalar_tensor_tensor(
-                    out=mixed[:, n, :], in0=y_flat, scalar=weight, in1=mixed[:, n, :],
+                    out=mixed[:, n, :], in0=y, scalar=weight, in1=before,
                     op0=ALU.mult, op1=ALU.add,
                 )
             if e == EXPERTS - 1 and n % 4 == 3:
                 nc.sync.dma_start(out=out[:, n - 3 : n + 1, :], in_=mixed[:, n - 3 : n + 1, :])
 
-        def schedule_expert(step, e, z):
-            y = small.tile(shape_gi, F32)
-            group_max = small.tile([P, GROUPS], F32)
-            group_sum = small.tile([P, GROUPS], F32)
-            at(step, lambda: nc.vector.tensor_tensor(
-                out=y[:].rearrange("p g i -> p (g i)"), in0=z[:], in1=bias_all[:, e, :], op=ALU.add))
-            at(step + 1, lambda: nc.vector.tensor_reduce(
-                out=group_max[:], in_=y[:], axis=AXIS_X, op=ALU.max))
-            at(step + 2, lambda: nc.vector.tensor_tensor(
-                out=y[:], in0=y[:], in1=group_max[:].unsqueeze(2).to_broadcast(shape_gi),
-                op=ALU.subtract))
-            at(step + 4, lambda: nc.scalar.activation(out=y[:], in_=y[:], func=ACT.Exp))
-            at(step + 6, lambda: nc.vector.tensor_reduce(
-                out=group_sum[:], in_=y[:], axis=AXIS_X, op=ALU.add))
-            at(step + 7, lambda: nc.vector.reciprocal(out=group_sum[:], in_=group_sum[:]))
-            at(step + 8, lambda: nc.vector.tensor_tensor(
-                out=y[:], in0=y[:], in1=group_sum[:].unsqueeze(2).to_broadcast(shape_gi),
-                op=ALU.mult))
-            for n in range(AGENTS):
-                at(step + 9 + n, lambda n=n: mix(e, n, y))
+        def product(e, n, y, products):
+            nc.scalar.activation(
+                out=products[:, n, :], in_=y, func=ACT.Copy, scale=comb[:, n, e : e + 1]
+            )
+
+        def add_products(e, products):
+            nc.tensor.matmul(
+                out=psum_mixed[:].rearrange("p n l -> p (n l)"),
+                lhsT=identity[:],
+                rhs=products[:].rearrange("p n l -> p (n l)"),
+                start=(e == 0),
+                stop=(e == EXPERTS - 2),
+            )
+
+        def schedule_experts(step, experts, z):
+            count = len(experts)
+            is_last = experts[-1] == EXPERTS - 1
+            groups = count * GROUPS
+            bias = bias_all[:, experts[0] : experts[0] + count, :]
+            y = small.tile([P, groups, SIMNORM], F32)
+            y_by_expert = y[:].rearrange("p (e g) i -> p e (g i)", e=count)
+            z_groups = z[:].rearrange("p e (g i) -> p (e g) i", i=SIMNORM)
+            bias_groups = bias.rearrange("p e (g i) -> p (e g) i", i=SIMNORM)
+            group_max = small.tile([P, groups], F32)
+            group_sum = small.tile([P, groups], F32)
+            pieces = 2 if is_last else 1
+            size = groups // pieces
+            shape = [P, size, SIMNORM]
+            for j in range(pieces):
+                g = slice(j * size, (j + 1) * size)
+                at(step, lambda g=g: nc.vector.tensor_tensor(
+                    out=y[:, g, :], in0=z_groups[:, g, :], in1=bias_groups[:, g, :], op=ALU.add))
+                at(step + 1, lambda g=g: nc.vector.tensor_reduce(
+                    out=group_max[:, g], in_=y[:, g, :], axis=AXIS_X, op=ALU.max))
+                at(step + 2, lambda g=g: nc.vector.tensor_tensor(
+                    out=y[:, g, :], in0=y[:, g, :],
+                    in1=group_max[:, g].unsqueeze(2).to_broadcast(shape), op=ALU.subtract))
+                at(step + 4, lambda g=g: nc.scalar.activation(
+                    out=y[:, g, :], in_=y[:, g, :], func=ACT.Exp))
+                at(step + 5, lambda g=g: nc.vector.tensor_reduce(
+                    out=group_sum[:, g], in_=y[:, g, :], axis=AXIS_X, op=ALU.add))
+                at(step + 6, lambda g=g: nc.vector.reciprocal(
+                    out=group_sum[:, g], in_=group_sum[:, g]))
+                at(step + 7, lambda g=g: nc.vector.tensor_tensor(
+                    out=y[:, g, :], in0=y[:, g, :],
+                    in1=group_sum[:, g].unsqueeze(2).to_broadcast(shape), op=ALU.mult))
+            first_on_vector = 0 if is_last else PSUM_AGENTS
+            on_vector = AGENTS - first_on_vector
+            for j, e in enumerate(experts):
+                y_e = y_by_expert[:, j, :]
+                for n in range(first_on_vector, AGENTS):
+                    order = j * on_vector + n - first_on_vector
+                    at(step + 8 + order // MIXES_PER_STEP, lambda e=e, n=n, y_e=y_e: mix(e, n, y_e))
+                if not is_last:
+                    products = small.tile([P, PSUM_AGENTS, FEATURES], F32)
+                    for n in range(PSUM_AGENTS):
+                        at(
+                            step + 8 + j * PSUM_AGENTS + n,
+                            lambda e=e, n=n, y_e=y_e, products=products: product(e, n, y_e, products),
+                        )
+                    at(
+                        step + 8 + (j + 1) * PSUM_AGENTS,
+                        lambda e=e, products=products: add_products(e, products),
+                    )
 
         schedule_comb(2)
         at(4, lambda: spread_bias(0))
@@ -223,15 +272,17 @@ def tile_softmoedynamics_pb_k_kernel(tc, h2, logits, W3, b3, out):
         ready = {}
         operands = {}
         sums = {}
+        set_of = {e: experts for experts in EXPERT_SETS for e in experts}
         for i in range(len(units) + 2):
             if i >= 2:
                 e, c0, n = units[i - 2]
-                if c0 == 0:
-                    z = psum_z.tile([P, FEATURES], F32, name="z")
-                    sums[e] = z
-                multiply(i - 2, sums[e], *operands[i - 2])
-                if c0 + n == HIDDEN // K_PASS:
-                    schedule_expert(2 * i + 1, e, sums[e])
+                experts = set_of[e]
+                if c0 == 0 and e == experts[0]:
+                    z = psum_z.tile([P, len(experts), FEATURES], F32, name="z")
+                    sums[experts] = z
+                multiply(i - 2, sums[experts][:, e - experts[0], :], *operands[i - 2])
+                if c0 + n == HIDDEN // K_PASS and e == experts[-1]:
+                    schedule_experts(2 * i + 1, experts, sums[experts])
             if i + 1 < len(units):
                 if i + 1 not in loaded:
                     loaded[i + 1] = load(i + 1)

@@ -20,14 +20,14 @@ BATCH, AGENTS, EXPERTS, FEATURES, HIDDEN = 128, 8, 8, 128, 8192
 SIMNORM = 8
 GROUPS = FEATURES // SIMNORM
 
-EXPERT_SETS = ((0, 1), (2, 3), (4, 5), (6,), (7,))
+EXPERT_SETS = tuple((e,) for e in range(EXPERTS))
 PSUM_AGENTS = 4
-MIXES_PER_STEP = 2
 
 FIRST_EXPERT_UNITS = (2, 2, 4, 4, 4)
 EXPERT_UNITS = (4, 4, 4, 4)
 LAST_EXPERT_UNITS = (4, 4, 4, 2, 2)
-VECTOR_COLUMNS = 76
+VECTOR_COLUMNS = 72
+LOADS_AHEAD = 4
 BANK_PASSES = 2
 
 FLOPS = 2 * BATCH * EXPERTS * HIDDEN * FEATURES + 2 * BATCH * AGENTS * EXPERTS * FEATURES
@@ -55,6 +55,7 @@ def tile_softmoedynamics_pb_k_kernel(tc, h2, logits, W3, b3, out):
         ctx.enter_context(tc.manual_schedule())
         consts = ctx.enter_context(tc.tile_pool(name="consts", bufs=1))
         raw = ctx.enter_context(tc.tile_pool(name="raw", bufs=12))
+        raw_long = ctx.enter_context(tc.tile_pool(name="raw_long", bufs=6))
         grouped = ctx.enter_context(tc.tile_pool(name="grouped", bufs=4))
         quantised = ctx.enter_context(tc.tile_pool(name="quantised", bufs=4))
         small = ctx.enter_context(tc.tile_pool(name="small", bufs=3))
@@ -62,20 +63,34 @@ def tile_softmoedynamics_pb_k_kernel(tc, h2, logits, W3, b3, out):
         psum_mix = ctx.enter_context(tc.psum_pool(name="psum_mix", bufs=1))
         psum_z = ctx.enter_context(tc.psum_pool(name="psum_z", bufs=2))
 
-        def load(u):
+        def load_w(u):
             e, c0, n = units[u]
             k = slice(c0 * K_PASS, (c0 + n) * K_PASS)
             raw_w = raw.tile([P, n, PACK, FEATURES], BF16)
             nc.sync.dma_start(
                 out=raw_w[:], in_=W3[e, k, :].rearrange("(c p t) l -> p c t l", p=P, t=PACK)
             )
-            raw_h = raw.tile([P, n * K_PASS], BF16)
-            nc.sync.dma_start(out=raw_h[:], in_=h2[:, e, k])
-            return raw_h, raw_w
+            loaded_w[u] = raw_w
+
+        def load_h(first, count, queue):
+            e, c0 = units[first][0:2]
+            last = first + count - 1
+            c1 = units[last][1] + units[last][2]
+            raw_h = raw_long.tile([P, (c1 - c0) * K_PASS], BF16)
+            queue.dma_start(out=raw_h[:], in_=h2[:, e, c0 * K_PASS : c1 * K_PASS])
+            for u in range(first, first + count):
+                k0 = (units[u][1] - c0) * K_PASS
+                loaded_h[u] = raw_h[:, k0 : k0 + units[u][2] * K_PASS]
+
+        def long_load(u):
+            index = [v for v in range(len(units)) if units[v][0] == units[u][0]].index(u)
+            if index % 2 == 1:
+                return 0
+            return 2 if u + 1 < len(units) and units[u + 1][0] == units[u][0] else 1
 
         def transpose_h(u, raw_h):
             n = units[u][2]
-            words = raw_h[:].bitcast(F32).rearrange("p (c w v) -> p c v w", c=n, v=2)
+            words = raw_h.bitcast(F32).rearrange("p (c w v) -> p c v w", c=n, v=2)
             banks = []
             for c0 in range(0, n, BANK_PASSES):
                 bank = psum_t.tile([P, BANK_PASSES, 2, BATCH], F32, tag="bank")
@@ -134,7 +149,12 @@ def tile_softmoedynamics_pb_k_kernel(tc, h2, logits, W3, b3, out):
                     stop=(c0 + c == HIDDEN // K_PASS - 1),
                 )
 
-        loaded = {0: load(0), 1: load(1)}
+        loaded_w = {}
+        loaded_h = {}
+        first_units = len(FIRST_EXPERT_UNITS)
+        for u in range(LOADS_AHEAD):
+            load_w(u)
+            load_h(u, 1, nc.sync)
         logits_sb = consts.tile([P, AGENTS, EXPERTS], BF16)
         nc.sync.dma_start(out=logits_sb[:], in_=logits)
         identity = consts.tile([P, P], F32)
@@ -247,28 +267,28 @@ def tile_softmoedynamics_pb_k_kernel(tc, h2, logits, W3, b3, out):
                     out=y[:, g, :], in0=y[:, g, :],
                     in1=group_sum[:, g].unsqueeze(2).to_broadcast(shape), op=ALU.mult))
             first_on_vector = 0 if is_last else PSUM_AGENTS
-            on_vector = AGENTS - first_on_vector
             for j, e in enumerate(experts):
                 y_e = y_by_expert[:, j, :]
-                for n in range(first_on_vector, AGENTS):
-                    order = j * on_vector + n - first_on_vector
-                    at(step + 8 + order // MIXES_PER_STEP, lambda e=e, n=n, y_e=y_e: mix(e, n, y_e))
+                for n in range(PSUM_AGENTS, AGENTS):
+                    at(step + 8 + j, lambda e=e, n=n, y_e=y_e: mix(e, n, y_e))
+                for n in range(first_on_vector, PSUM_AGENTS):
+                    at(step + 8 + j, lambda e=e, n=n, y_e=y_e: mix(e, n, y_e))
                 if not is_last:
                     products = small.tile([P, PSUM_AGENTS, FEATURES], F32)
                     for n in range(PSUM_AGENTS):
                         at(
-                            step + 8 + j * PSUM_AGENTS + n,
+                            step + 8 + j,
                             lambda e=e, n=n, y_e=y_e, products=products: product(e, n, y_e, products),
                         )
                     at(
-                        step + 8 + (j + 1) * PSUM_AGENTS,
+                        step + 9 + j,
                         lambda e=e, products=products: add_products(e, products),
                     )
 
         schedule_comb(2)
         at(4, lambda: spread_bias(0))
         at(6, lambda: spread_bias(512))
-        banks = {0: transpose_h(0, loaded[0][0])}
+        banks = {0: transpose_h(0, loaded_h[0])}
         ready = {}
         operands = {}
         sums = {}
@@ -283,17 +303,22 @@ def tile_softmoedynamics_pb_k_kernel(tc, h2, logits, W3, b3, out):
                 multiply(i - 2, sums[experts][:, e - experts[0], :], *operands[i - 2])
                 if c0 + n == HIDDEN // K_PASS and e == experts[-1]:
                     schedule_experts(2 * i + 1, experts, sums[experts])
+            ahead = i + LOADS_AHEAD
+            if ahead < len(units):
+                load_w(ahead)
+                if ahead < first_units:
+                    load_h(ahead, 1, nc.sync)
             if i + 1 < len(units):
-                if i + 1 not in loaded:
-                    loaded[i + 1] = load(i + 1)
-                banks[i + 1] = transpose_h(i + 1, loaded[i + 1][0])
+                banks[i + 1] = transpose_h(i + 1, loaded_h[i + 1])
             if i < len(units):
                 values = grouped.tile([P, 2 * units[i][2] * K_PASS], BF16, align_bytes=64)
                 ready[i] = values
-                group_w(i, loaded[i][1], values)
+                group_w(i, loaded_w[i], values)
             run(2 * i)
             if i < len(units):
                 group_h(i, banks[i], ready[i])
+            if first_units <= ahead < len(units) and long_load(ahead) > 0:
+                load_h(ahead, long_load(ahead), nc.sync)
             if 1 <= i <= len(units):
                 operands[i - 1] = quantise(i - 1, ready[i - 1])
             run(2 * i + 1)

@@ -26,7 +26,9 @@ PSUM_AGENTS = 4
 FIRST_EXPERT_UNITS = (2, 2, 4, 4, 4)
 EXPERT_UNITS = (4, 4, 4, 4)
 LAST_EXPERT_UNITS = (4, 4, 4, 2, 2)
-VECTOR_COLUMNS = 72
+VECTOR_COLUMNS = 80
+VECTOR_COLUMNS_AT_END = 56
+UNITS_AT_END = 3
 LOADS_AHEAD = 4
 BANK_PASSES = 2
 
@@ -59,7 +61,8 @@ def tile_softmoedynamics_pb_k_kernel(tc, h2, logits, W3, b3, out):
         grouped = ctx.enter_context(tc.tile_pool(name="grouped", bufs=4))
         quantised = ctx.enter_context(tc.tile_pool(name="quantised", bufs=4))
         small = ctx.enter_context(tc.tile_pool(name="small", bufs=3))
-        psum_t = ctx.enter_context(tc.psum_pool(name="psum_t", bufs=5))
+        psum_t = ctx.enter_context(tc.psum_pool(name="psum_t", bufs=4))
+        psum_spare = ctx.enter_context(tc.psum_pool(name="psum_spare", bufs=1))
         psum_mix = ctx.enter_context(tc.psum_pool(name="psum_mix", bufs=1))
         psum_z = ctx.enter_context(tc.psum_pool(name="psum_z", bufs=2))
 
@@ -83,6 +86,8 @@ def tile_softmoedynamics_pb_k_kernel(tc, h2, logits, W3, b3, out):
                 loaded_h[u] = raw_h[:, k0 : k0 + units[u][2] * K_PASS]
 
         def long_load(u):
+            if units[u][0] == EXPERTS - 1:
+                return 1
             index = [v for v in range(len(units)) if units[v][0] == units[u][0]].index(u)
             if index % 2 == 1:
                 return 0
@@ -114,7 +119,7 @@ def tile_softmoedynamics_pb_k_kernel(tc, h2, logits, W3, b3, out):
 
         def group_w(u, raw_w, values):
             n = units[u][2]
-            v = VECTOR_COLUMNS
+            v = VECTOR_COLUMNS if u < len(units) - UNITS_AT_END else VECTOR_COLUMNS_AT_END
             grouped_w = values[:, n * K_PASS : 2 * n * K_PASS].rearrange(
                 "p (c l t) -> p c l t", c=n, t=PACK
             )
@@ -148,7 +153,18 @@ def tile_softmoedynamics_pb_k_kernel(tc, h2, logits, W3, b3, out):
                     start=(c0 + c == 0),
                     stop=(c0 + c == HIDDEN // K_PASS - 1),
                 )
+            w_cols = slice(n * P, 2 * n * P)
+            nc.tensor.matmul_mx(
+                out=spare[:, 0 : n * P],
+                lhsT=codes[:, 0:P].bitcast(FP8X4),
+                lhsT_scale=scales[:, 0:P],
+                rhs=codes[:, w_cols].bitcast(FP8X4),
+                rhs_scale=scales[:, w_cols],
+                start=True,
+                stop=True,
+            )
 
+        spare = psum_spare.tile([P, 512], F32)
         loaded_w = {}
         loaded_h = {}
         first_units = len(FIRST_EXPERT_UNITS)
@@ -177,12 +193,11 @@ def tile_softmoedynamics_pb_k_kernel(tc, h2, logits, W3, b3, out):
         psum_mixed = psum_mix.tile([P, PSUM_AGENTS, FEATURES], F32)
 
         def spread_bias(n0):
-            bias_bank = psum_t.tile([P, 512], F32, tag="bank")
             nc.tensor.matmul(
-                out=bias_bank[:], lhsT=ones[:], rhs=bias_row[:, n0 : n0 + 512], start=True, stop=True
+                out=spare[:], lhsT=ones[:], rhs=bias_row[:, n0 : n0 + 512], start=True, stop=True
             )
             bias_flat = bias_all[:].rearrange("p e l -> p (e l)")
-            nc.scalar.copy(out=bias_flat[:, n0 : n0 + 512], in_=bias_bank[:])
+            nc.scalar.copy(out=bias_flat[:, n0 : n0 + 512], in_=spare[:])
 
         later = {}
 
@@ -217,8 +232,8 @@ def tile_softmoedynamics_pb_k_kernel(tc, h2, logits, W3, b3, out):
                     out=mixed[:, n, :], in0=y, scalar=weight, in1=before,
                     op0=ALU.mult, op1=ALU.add,
                 )
-            if e == EXPERTS - 1 and n % 4 == 3:
-                nc.sync.dma_start(out=out[:, n - 3 : n + 1, :], in_=mixed[:, n - 3 : n + 1, :])
+            if e == EXPERTS - 1 and n % 2 == 1:
+                nc.sync.dma_start(out=out[:, n - 1 : n + 1, :], in_=mixed[:, n - 1 : n + 1, :])
 
         def product(e, n, y, products):
             nc.scalar.activation(

from contextlib import ExitStack

import concourse.mybir as mybir
from concourse.masks import make_identity

F32 = mybir.dt.float32
BF16 = mybir.dt.bfloat16
U32 = mybir.dt.uint32
U8 = mybir.dt.uint8
FP8X4 = mybir.dt.float8_e4m3fn_x4
ALU = mybir.AluOpType
ACT = mybir.ActivationFunctionType
AXIS_X = mybir.AxisListType.X

P = 128
PACK = 4
K_PASS = P * PACK

BATCH, AGENTS, EXPERTS, FEATURES, HIDDEN = 128, 8, 8, 128, 8192
SIMNORM = 8
GROUPS = FEATURES // SIMNORM

EXPERT_SETS = tuple((e,) for e in range(EXPERTS))
PSUM_AGENTS = 4

FIRST_EXPERT_UNITS = (2, 2, 4, 4, 4)
EXPERT_UNITS = (4, 4, 4, 4)
LAST_EXPERT_UNITS = (4, 4, 4, 2, 2)
VECTOR_COLUMNS = 80
VECTOR_COLUMNS_AT_END = 56
UNITS_AT_END = 3
LOADS_AHEAD = 4
BANK_PASSES = 2

FLOPS = 2 * BATCH * EXPERTS * HIDDEN * FEATURES + 2 * BATCH * AGENTS * EXPERTS * FEATURES


def list_units():
    units = []
    for e in range(EXPERTS):
        sizes = EXPERT_UNITS
        if e == 0:
            sizes = FIRST_EXPERT_UNITS
        if e == EXPERTS - 1:
            sizes = LAST_EXPERT_UNITS
        c0 = 0
        for n in sizes:
            units.append((e, c0, n))
            c0 += n
    return units


def tile_softmoedynamics_pb_k_kernel(tc, h2, logits, W3, b3, out):
    nc = tc.nc
    units = list_units()
    with ExitStack() as ctx:
        ctx.enter_context(tc.manual_schedule())
        consts = ctx.enter_context(tc.tile_pool(name="consts", bufs=1))
        raw = ctx.enter_context(tc.tile_pool(name="raw", bufs=12))
        raw_long = ctx.enter_context(tc.tile_pool(name="raw_long", bufs=6))
        grouped = ctx.enter_context(tc.tile_pool(name="grouped", bufs=4))
        quantised = ctx.enter_context(tc.tile_pool(name="quantised", bufs=4))
        small = ctx.enter_context(tc.tile_pool(name="small", bufs=3))
        psum_t = ctx.enter_context(tc.psum_pool(name="psum_t", bufs=4))
        psum_spare = ctx.enter_context(tc.psum_pool(name="psum_spare", bufs=1))
        psum_mix = ctx.enter_context(tc.psum_pool(name="psum_mix", bufs=1))
        psum_z = ctx.enter_context(tc.psum_pool(name="psum_z", bufs=2))

        def load_w(u):
            e, c0, n = units[u]
            k = slice(c0 * K_PASS, (c0 + n) * K_PASS)
            raw_w = raw.tile([P, n, PACK, FEATURES], BF16)
            nc.sync.dma_start(
                out=raw_w[:], in_=W3[e, k, :].rearrange("(c p t) l -> p c t l", p=P, t=PACK)
            )
            loaded_w[u] = raw_w

        def load_h(first, count, queue):
            e, c0 = units[first][0:2]
            last = first + count - 1
            c1 = units[last][1] + units[last][2]
            raw_h = raw_long.tile([P, (c1 - c0) * K_PASS], BF16)
            queue.dma_start(out=raw_h[:], in_=h2[:, e, c0 * K_PASS : c1 * K_PASS])
            for u in range(first, first + count):
                k0 = (units[u][1] - c0) * K_PASS
                loaded_h[u] = raw_h[:, k0 : k0 + units[u][2] * K_PASS]

        def long_load(u):
            if units[u][0] == EXPERTS - 1:
                return 1
            index = [v for v in range(len(units)) if units[v][0] == units[u][0]].index(u)
            if index % 2 == 1:
                return 0
            return 2 if u + 1 < len(units) and units[u + 1][0] == units[u][0] else 1

        def transpose_h(u, raw_h):
            n = units[u][2]
            words = raw_h.bitcast(F32).rearrange("p (c w v) -> p c v w", c=n, v=2)
            banks = []
            for c0 in range(0, n, BANK_PASSES):
                bank = psum_t.tile([P, BANK_PASSES, 2, BATCH], F32, tag="bank")
                for c in range(BANK_PASSES):
                    for v in range(2):
                        nc.tensor.transpose(bank[:, c, v, :], words[:, c0 + c, v, :], identity[:])
                banks.append(bank)
            return banks

        def group_h(u, banks, values):
            n = units[u][2]
            grouped_words = values[:, 0 : n * K_PASS].bitcast(F32).rearrange(
                "p (c b v) -> p c b v", c=n, v=2
            )
            for j in range(len(banks)):
                c0 = j * BANK_PASSES
                nc.scalar.copy(
                    out=grouped_words[:, c0 : c0 + BANK_PASSES, :, :],
                    in_=banks[j][:].rearrange("p c v b -> p c b v"),
                )

        def group_w(u, raw_w, values):
            n = units[u][2]
            v = VECTOR_COLUMNS if u < len(units) - UNITS_AT_END else VECTOR_COLUMNS_AT_END
            grouped_w = values[:, n * K_PASS : 2 * n * K_PASS].rearrange(
                "p (c l t) -> p c l t", c=n, t=PACK
            )
            nc.vector.tensor_copy(
                out=grouped_w[:, :, 0:v, :].rearrange("p c (q i) t -> p c q t i", i=4),
                in_=raw_w[:, :, :, 0:v].rearrange("p c t (q i) -> p c q t i", i=4),
            )
            nc.scalar.copy(
                out=grouped_w[:, :, v:FEATURES, :].rearrange("p c (q i) t -> p c q t i", i=4),
                in_=raw_w[:, :, :, v:FEATURES].rearrange("p c t (q i) -> p c q t i", i=4),
            )

        def quantise(u, values):
            n = units[u][2]
            codes = quantised.tile([P, 2 * n * P], U32, align_bytes=64)
            scales = quantised.tile([P, 2 * n * P], U8, align_bytes=64)
            nc.vector.quantize_mx(out=codes[:].bitcast(FP8X4), scales=scales[:], in_=values[:])
            return codes, scales

        def multiply(u, z, codes, scales):
            e, c0, n = units[u]
            for c in range(n):
                h_cols = slice(c * P, (c + 1) * P)
                w_cols = slice((n + c) * P, (n + c + 1) * P)
                nc.tensor.matmul_mx(
                    out=z,
                    lhsT=codes[:, h_cols].bitcast(FP8X4),
                    lhsT_scale=scales[:, h_cols],
                    rhs=codes[:, w_cols].bitcast(FP8X4),
                    rhs_scale=scales[:, w_cols],
                    start=(c0 + c == 0),
                    stop=(c0 + c == HIDDEN // K_PASS - 1),
                )
            w_cols = slice(n * P, 2 * n * P)
            nc.tensor.matmul_mx(
                out=spare[:, 0 : n * P],
                lhsT=codes[:, 0:P].bitcast(FP8X4),
                lhsT_scale=scales[:, 0:P],
                rhs=codes[:, w_cols].bitcast(FP8X4),
                rhs_scale=scales[:, w_cols],
                start=True,
                stop=True,
            )

        spare = psum_spare.tile([P, 512], F32)
        loaded_w = {}
        loaded_h = {}
        first_units = len(FIRST_EXPERT_UNITS)
        for u in range(LOADS_AHEAD):
            load_w(u)
            load_h(u, 1, nc.sync)
        logits_sb = consts.tile([P, AGENTS, EXPERTS], BF16)
        nc.sync.dma_start(out=logits_sb[:], in_=logits)
        identity = consts.tile([P, P], F32)
        make_identity(nc, identity[:])
        warm = consts.tile([P, 1], F32)
        nc.gpsimd.memset(warm[:], 0.0)
        nc.scalar.activation(out=warm[:], in_=warm[:], func=ACT.Exp)
        bias_row = consts.tile([P, EXPERTS * FEATURES], BF16)
        nc.gpsimd.memset(bias_row[:], 0.0)
        nc.sync.dma_start(out=bias_row[0:1, :], in_=b3.rearrange("(o e) l -> o (e l)", o=1))
        ones = consts.tile([P, P], BF16)
        nc.gpsimd.memset(ones[:], 1.0)

        bias_all = consts.tile([P, EXPERTS, FEATURES], F32)
        shape_ne = [P, AGENTS, EXPERTS]
        logit_max = consts.tile([P, AGENTS], F32)
        comb = consts.tile(shape_ne, F32)
        logit_sum = consts.tile([P, AGENTS], F32)
        mixed = consts.tile([P, AGENTS, FEATURES], F32)
        psum_mixed = psum_mix.tile([P, PSUM_AGENTS, FEATURES], F32)

        def spread_bias(n0):
            nc.tensor.matmul(
                out=spare[:], lhsT=ones[:], rhs=bias_row[:, n0 : n0 + 512], start=True, stop=True
            )
            bias_flat = bias_all[:].rearrange("p e l -> p (e l)")
            nc.scalar.copy(out=bias_flat[:, n0 : n0 + 512], in_=spare[:])

        later = {}

        def at(step, function):
            later.setdefault(step, []).append(function)

        def run(step):
            for function in later.get(step, []):
                function()

        def schedule_comb(step):
            at(step, lambda: nc.vector.tensor_reduce(
                out=logit_max[:], in_=logits_sb[:], axis=AXIS_X, op=ALU.max))
            at(step + 1, lambda: nc.vector.tensor_tensor(
                out=comb[:], in0=logits_sb[:], in1=logit_max[:].unsqueeze(2).to_broadcast(shape_ne),
                op=ALU.subtract))
            at(step + 3, lambda: nc.scalar.activation(out=comb[:], in_=comb[:], func=ACT.Exp))
            at(step + 5, lambda: nc.vector.tensor_reduce(
                out=logit_sum[:], in_=comb[:], axis=AXIS_X, op=ALU.add))
            at(step + 6, lambda: nc.vector.reciprocal(out=logit_sum[:], in_=logit_sum[:]))
            at(step + 7, lambda: nc.vector.tensor_tensor(
                out=comb[:], in0=comb[:], in1=logit_sum[:].unsqueeze(2).to_broadcast(shape_ne),
                op=ALU.mult))

        def mix(e, n, y):
            weight = comb[:, n, e : e + 1]
            if e == 0:
                nc.vector.tensor_scalar_mul(out=mixed[:, n, :], in0=y, scalar1=weight)
            else:
                before = psum_mixed[:, n, :] if n < PSUM_AGENTS else mixed[:, n, :]
                nc.vector.scalar_tensor_tensor(
                    out=mixed[:, n, :], in0=y, scalar=weight, in1=before,
                    op0=ALU.mult, op1=ALU.add,
                )
            if e == EXPERTS - 1 and n % 2 == 1:
                nc.sync.dma_start(out=out[:, n - 1 : n + 1, :], in_=mixed[:, n - 1 : n + 1, :])

        def product(e, n, y, products):
            nc.scalar.activation(
                out=products[:, n, :], in_=y, func=ACT.Copy, scale=comb[:, n, e : e + 1]
            )

        def add_products(e, products):
            nc.tensor.matmul(
                out=psum_mixed[:].rearrange("p n l -> p (n l)"),
                lhsT=identity[:],
                rhs=products[:].rearrange("p n l -> p (n l)"),
                start=(e == 0),
                stop=(e == EXPERTS - 2),
            )

        def schedule_experts(step, experts, z):
            count = len(experts)
            is_last = experts[-1] == EXPERTS - 1
            groups = count * GROUPS
            bias = bias_all[:, experts[0] : experts[0] + count, :]
            y = small.tile([P, groups, SIMNORM], F32)
            y_by_expert = y[:].rearrange("p (e g) i -> p e (g i)", e=count)
            z_groups = z[:].rearrange("p e (g i) -> p (e g) i", i=SIMNORM)
            bias_groups = bias.rearrange("p e (g i) -> p (e g) i", i=SIMNORM)
            group_max = small.tile([P, groups], F32)
            group_sum = small.tile([P, groups], F32)
            pieces = 2 if is_last else 1
            size = groups // pieces
            shape = [P, size, SIMNORM]
            for j in range(pieces):
                g = slice(j * size, (j + 1) * size)
                at(step, lambda g=g: nc.vector.tensor_tensor(
                    out=y[:, g, :], in0=z_groups[:, g, :], in1=bias_groups[:, g, :], op=ALU.add))
                at(step + 1, lambda g=g: nc.vector.tensor_reduce(
                    out=group_max[:, g], in_=y[:, g, :], axis=AXIS_X, op=ALU.max))
                at(step + 2, lambda g=g: nc.vector.tensor_tensor(
                    out=y[:, g, :], in0=y[:, g, :],
                    in1=group_max[:, g].unsqueeze(2).to_broadcast(shape), op=ALU.subtract))
                at(step + 4, lambda g=g: nc.scalar.activation(
                    out=y[:, g, :], in_=y[:, g, :], func=ACT.Exp))
                at(step + 5, lambda g=g: nc.vector.tensor_reduce(
                    out=group_sum[:, g], in_=y[:, g, :], axis=AXIS_X, op=ALU.add))
                at(step + 6, lambda g=g: nc.vector.reciprocal(
                    out=group_sum[:, g], in_=group_sum[:, g]))
                at(step + 7, lambda g=g: nc.vector.tensor_tensor(
                    out=y[:, g, :], in0=y[:, g, :],
                    in1=group_sum[:, g].unsqueeze(2).to_broadcast(shape), op=ALU.mult))
            first_on_vector = 0 if is_last else PSUM_AGENTS
            for j, e in enumerate(experts):
                y_e = y_by_expert[:, j, :]
                for n in range(PSUM_AGENTS, AGENTS):
                    at(step + 8 + j, lambda e=e, n=n, y_e=y_e: mix(e, n, y_e))
                for n in range(first_on_vector, PSUM_AGENTS):
                    at(step + 8 + j, lambda e=e, n=n, y_e=y_e: mix(e, n, y_e))
                if not is_last:
                    products = small.tile([P, PSUM_AGENTS, FEATURES], F32)
                    for n in range(PSUM_AGENTS):
                        at(
                            step + 8 + j,
                            lambda e=e, n=n, y_e=y_e, products=products: product(e, n, y_e, products),
                        )
                    at(
                        step + 9 + j,
                        lambda e=e, products=products: add_products(e, products),
                    )

        schedule_comb(2)
        at(4, lambda: spread_bias(0))
        at(6, lambda: spread_bias(512))
        banks = {0: transpose_h(0, loaded_h[0])}
        ready = {}
        operands = {}
        sums = {}
        set_of = {e: experts for experts in EXPERT_SETS for e in experts}
        for i in range(len(units) + 2):
            if i >= 2:
                e, c0, n = units[i - 2]
                experts = set_of[e]
                if c0 == 0 and e == experts[0]:
                    z = psum_z.tile([P, len(experts), FEATURES], F32, name="z")
                    sums[experts] = z
                multiply(i - 2, sums[experts][:, e - experts[0], :], *operands[i - 2])
                if c0 + n == HIDDEN // K_PASS and e == experts[-1]:
                    schedule_experts(2 * i + 1, experts, sums[experts])
            ahead = i + LOADS_AHEAD
            if ahead < len(units):
                load_w(ahead)
                if ahead < first_units:
                    load_h(ahead, 1, nc.sync)
            if i + 1 < len(units):
                banks[i + 1] = transpose_h(i + 1, loaded_h[i + 1])
            if i < len(units):
                values = grouped.tile([P, 2 * units[i][2] * K_PASS], BF16, align_bytes=64)
                ready[i] = values
                group_w(i, loaded_w[i], values)
            run(2 * i)
            if i < len(units):
                group_h(i, banks[i], ready[i])
            if first_units <= ahead < len(units) and long_load(ahead) > 0:
                load_h(ahead, long_load(ahead), nc.sync)
            if 1 <= i <= len(units):
                operands[i - 1] = quantise(i - 1, ready[i - 1])
            run(2 * i + 1)
        for step in range(2 * (len(units) + 2), max(later) + 1):
            run(step)
